import numpy as np
import ml_dtypes

BF16 = ml_dtypes.bfloat16


def bf(x):
    return np.asarray(x, np.float32).astype(BF16)


def f32(x):
    return np.asarray(x, np.float32)


def f64(x):
    return np.asarray(x).astype(np.float64)


def striped(idx):
    return np.tile(idx.reshape(-1, 16).T, (8, 1))


E, S, N, D, M, H, K = 512, 2048, 8192, 3, 256, 1024, 8


def setup_inputs():
    return {
        "table": f32(np.random.standard_normal((E, S))),
        "w": bf(np.random.standard_normal((2 * E, E)) / np.sqrt(E)),
        "w_b": f32(0.1 * np.random.standard_normal((E, 1))),
        "p_w": bf(np.random.standard_normal((E, M)) / np.sqrt(E)),
        "p_b": f32(0.1 * np.random.standard_normal((M, 1))),
        "offs": striped(np.concatenate([np.random.permutation(S)[:H] for _ in range(K)])),
    }


def reference(table, w, w_b, p_w, p_b, offs):
    idx = offs[:16].T.reshape(-1)
    r = np.maximum(f64(table), 0.0)
    pt = np.concatenate([f64(w)[:E], f64(w)[E:]], axis=1).T @ r
    half = N // 2
    u = pt[:E][:, idx[:half]] + f64(w_b)
    h = np.maximum(pt[E:][:, idx[half:]] + u, 0.0)
    hs = [h]
    for _ in range(D - 1):
        half = h.shape[1] // 2
        h = np.maximum(f64(w).T @ np.concatenate([h[:, :half], h[:, half:]], axis=0) + f64(w_b), 0.0)
        hs.append(h)
    return f64(p_w).T @ np.concatenate(hs, axis=1) + f64(p_b)

@@ -1,0 +1,146 @@
+import concourse.mybir as mybir
+
+F32 = mybir.dt.float32
+BF16 = mybir.dt.bfloat16
+U16 = mybir.dt.uint16
+ADD = mybir.AluOpType.add
+FUNC = mybir.ActivationFunctionType
+
+P = 128
+E = 512
+S = 2048
+N = 8192
+M = 256
+CH = 512
+EB = E // P
+MB = M // P
+SB = S // CH
+H1, H2, H3 = N // 2, N // 4, N // 8
+
+FLOPS = 2 * (2 * E * E * (S + H2 + H3) + E * M * (H1 + H2 + H3))
+
+
+def tile_recursivenn_b_kernel(tc, table, w, w_b, p_w, p_b, offs, out):
+    nc = tc.nc
+    with (
+        tc.tile_pool(name="held", bufs=1) as held,
+        tc.tile_pool(name="loaded", bufs=8) as loaded,
+        tc.tile_pool(name="left_sums", bufs=10) as left_sums,
+        tc.tile_pool(name="pair_sums", bufs=4) as pair_sums,
+        tc.tile_pool(name="results", bufs=6) as results,
+        tc.psum_pool(name="banks", bufs=8) as banks,
+    ):
+        w_blocks = [held.tile([P, E], BF16, name=f"w{k}") for k in range(2 * EB)]
+        for k in range(EB):
+            nc.scalar.dma_start(w_blocks[k][:], w[k * P : (k + 1) * P, :])
+
+        r = [[held.tile([P, CH], BF16, name=f"r{k}_{s}") for s in range(SB)] for k in range(EB)]
+        for s in range(SB):
+            for k in range(EB):
+                raw = loaded.tile([P, CH], F32, name="raw")
+                nc.sync.dma_start(raw[:], table[k * P : (k + 1) * P, s * CH : (s + 1) * CH])
+                nc.vector.tensor_scalar_max(r[k][s][:], raw[:], 0.0)
+
+        offsets = held.tile([P, N // 16], U16, name="offsets")
+        nc.sync.dma_start(offsets[:], offs)
+        for k in range(EB, 2 * EB):
+            nc.sync.dma_start(w_blocks[k][:], w[k * P : (k + 1) * P, :])
+        pw_blocks = [held.tile([P, M], BF16, name=f"pw{k}") for k in range(EB)]
+        for k in range(EB):
+            nc.sync.dma_start(pw_blocks[k][:], p_w[k * P : (k + 1) * P, :])
+
+        wb = [held.tile([P, 1], F32, name=f"wb{c}") for c in range(EB)]
+        for c in range(EB):
+            nc.gpsimd.dma_start(wb[c][:], w_b[c * P : (c + 1) * P, :])
+        pb = [held.tile([P, 1], F32, name=f"pb{m}") for m in range(MB)]
+        for m in range(MB):
+            nc.gpsimd.dma_start(pb[m][:], p_b[m * P : (m + 1) * P, :])
+        wb_wide = [held.tile([P, CH], F32, name=f"wb_wide{c}") for c in range(EB)]
+        for c in range(EB):
+            nc.vector.tensor_copy(wb_wide[c][:], wb[c][:].to_broadcast([P, CH]))
+
+        pt = [[held.tile([P, S], F32, name=f"pt{a}_{c}") for c in range(EB)] for a in range(2)]
+
+        for s in range(SB):
+            accs = [banks.tile([P, CH], F32, name="acc") for c in range(EB)]
+            for k in range(EB):
+                for c in range(EB):
+                    nc.tensor.matmul(
+                        accs[c][:],
+                        w_blocks[k][:, c * P : (c + 1) * P],
+                        r[k][s][:],
+                        start=(k == 0),
+                        stop=(k == EB - 1),
+                    )
+            for c in range(EB):
+                nc.scalar.activation(pt[0][c][:, s * CH : (s + 1) * CH], accs[c][:], FUNC.Copy)
+
+        for c in range(EB):
+            for s in range(SB):
+                acc = banks.tile([P, CH], F32, name="acc")
+                for k in range(EB):
+                    nc.tensor.matmul(
+                        acc[:],
+                        w_blocks[EB + k][:, c * P : (c + 1) * P],
+                        r[k][s][:],
+                        start=(k == 0),
+                        stop=(k == EB - 1),
+                    )
+                nc.scalar.activation(pt[1][c][:, s * CH : (s + 1) * CH], acc[:], FUNC.Copy)
+
+        h1 = [[held.tile([P, CH], BF16, name=f"h1_{g}_{e}") for e in range(EB)] for g in range(H1 // CH)]
+        h2 = [[held.tile([P, CH], BF16, name=f"h2_{g}_{e}") for e in range(EB)] for g in range(H2 // CH)]
+        h3 = [[held.tile([P, CH], BF16, name=f"h3_{g}_{e}") for e in range(EB)] for g in range(H3 // CH)]
+
+        def look_up(g, c):
+            first = g * CH // 16
+            left_entries = offsets[:, first : first + CH // 16]
+            right_entries = offsets[:, H1 // 16 + first : H1 // 16 + first + CH // 16]
+            u = left_sums.tile([P, CH], F32, name="u")
+            nc.vector.tensor_tensor(u[:], pt[0][c][:].indirect(left_entries), wb_wide[c][:], ADD)
+            pair = pair_sums.tile([P, CH], F32, name="pair")
+            nc.vector.tensor_tensor(pair[:], pt[1][c][:].indirect(right_entries), u[:], ADD)
+            nc.scalar.activation(h1[g][c][:], pair[:], FUNC.Relu)
+
+        def combine(left, right, parent):
+            accs = [banks.tile([P, CH], F32, name="acc") for c in range(EB)]
+            for e in range(EB):
+                for side, child in enumerate((left[e], right[e])):
+                    for c in range(EB):
+                        nc.tensor.matmul(
+                            accs[c][:],
+                            w_blocks[side * EB + e][:, c * P : (c + 1) * P],
+                            child[:],
+                            start=(e == 0 and side == 0),
+                            stop=(e == EB - 1 and side == 1),
+                        )
+            for c in range(EB):
+                nc.scalar.activation(parent[c][:], accs[c][:], FUNC.Relu, bias=wb[c][:])
+
+        def classify(nodes, first_column):
+            for m in range(MB):
+                acc = banks.tile([P, CH], F32, name="acc")
+                for e in range(EB):
+                    nc.tensor.matmul(
+                        acc[:],
+                        pw_blocks[e][:, m * P : (m + 1) * P],
+                        nodes[e][:],
+                        start=(e == 0),
+                        stop=(e == EB - 1),
+                    )
+                scores = results.tile([P, CH], F32, name="scores")
+                nc.scalar.activation(scores[:], acc[:], FUNC.Identity, bias=pb[m][:])
+                nc.sync.dma_start(out[m * P : (m + 1) * P, first_column : first_column + CH], scores[:])
+
+        for t in range(H3 // CH):
+            for q in (t, t + H3 // CH):
+                for c in range(EB):
+                    look_up(q, c)
+                    look_up(q + H2 // CH, c)
+                combine(h1[q], h1[q + H2 // CH], h2[q])
+                classify(h1[q], q * CH)
+                classify(h1[q + H2 // CH], (q + H2 // CH) * CH)
+            combine(h2[t], h2[t + H3 // CH], h3[t])
+            classify(h2[t], H1 + t * CH)
+            classify(h2[t + H3 // CH], H1 + (t + H3 // CH) * CH)
+            classify(h3[t], H1 + H2 + t * CH)

@@ -16,6 +16,7 @@ EB = E // P
 MB = M // P
 SB = S // CH
 H1, H2, H3 = N // 2, N // 4, N // 8
+G1, G2, G3 = H1 // CH, H2 // CH, H3 // CH
 
 FLOPS = 2 * (2 * E * E * (S + H2 + H3) + E * M * (H1 + H2 + H3))
 
@@ -24,14 +25,13 @@ def tile_recursivenn_b_kernel(tc, table, w, w_b, p_w, p_b, offs, out):
     nc = tc.nc
     with (
         tc.tile_pool(name="held", bufs=1) as held,
-        tc.tile_pool(name="loaded", bufs=8) as loaded,
-        tc.tile_pool(name="left_sums", bufs=10) as left_sums,
-        tc.tile_pool(name="pair_sums", bufs=4) as pair_sums,
+        tc.tile_pool(name="loaded", bufs=SB * EB) as loaded,
+        tc.tile_pool(name="sums", bufs=3) as sums,
         tc.tile_pool(name="results", bufs=6) as results,
         tc.psum_pool(name="banks", bufs=8) as banks,
     ):
         w_blocks = [held.tile([P, E], BF16, name=f"w{k}") for k in range(2 * EB)]
-        for k in range(EB):
+        for k in range(2 * EB):
             nc.scalar.dma_start(w_blocks[k][:], w[k * P : (k + 1) * P, :])
 
         r = [[held.tile([P, CH], BF16, name=f"r{k}_{s}") for s in range(SB)] for k in range(EB)]
@@ -43,79 +43,61 @@ def tile_recursivenn_b_kernel(tc, table, w, w_b, p_w, p_b, offs, out):
 
         offsets = held.tile([P, N // 16], U16, name="offsets")
         nc.sync.dma_start(offsets[:], offs)
-        for k in range(EB, 2 * EB):
-            nc.sync.dma_start(w_blocks[k][:], w[k * P : (k + 1) * P, :])
         pw_blocks = [held.tile([P, M], BF16, name=f"pw{k}") for k in range(EB)]
         for k in range(EB):
             nc.sync.dma_start(pw_blocks[k][:], p_w[k * P : (k + 1) * P, :])
 
         wb = [held.tile([P, 1], F32, name=f"wb{c}") for c in range(EB)]
         for c in range(EB):
-            nc.gpsimd.dma_start(wb[c][:], w_b[c * P : (c + 1) * P, :])
+            nc.scalar.dma_start(wb[c][:], w_b[c * P : (c + 1) * P, :])
         pb = [held.tile([P, 1], F32, name=f"pb{m}") for m in range(MB)]
         for m in range(MB):
-            nc.gpsimd.dma_start(pb[m][:], p_b[m * P : (m + 1) * P, :])
+            nc.scalar.dma_start(pb[m][:], p_b[m * P : (m + 1) * P, :])
         wb_wide = [held.tile([P, CH], F32, name=f"wb_wide{c}") for c in range(EB)]
         for c in range(EB):
             nc.vector.tensor_copy(wb_wide[c][:], wb[c][:].to_broadcast([P, CH]))
 
         pt = [[held.tile([P, S], F32, name=f"pt{a}_{c}") for c in range(EB)] for a in range(2)]
-
-        for s in range(SB):
-            accs = [banks.tile([P, CH], F32, name="acc") for c in range(EB)]
-            for k in range(EB):
-                for c in range(EB):
-                    nc.tensor.matmul(
-                        accs[c][:],
-                        w_blocks[k][:, c * P : (c + 1) * P],
-                        r[k][s][:],
-                        start=(k == 0),
-                        stop=(k == EB - 1),
-                    )
-            for c in range(EB):
-                nc.scalar.activation(pt[0][c][:, s * CH : (s + 1) * CH], accs[c][:], FUNC.Copy)
-
         for c in range(EB):
             for s in range(SB):
-                acc = banks.tile([P, CH], F32, name="acc")
-                for k in range(EB):
-                    nc.tensor.matmul(
-                        acc[:],
-                        w_blocks[EB + k][:, c * P : (c + 1) * P],
-                        r[k][s][:],
-                        start=(k == 0),
-                        stop=(k == EB - 1),
-                    )
-                nc.scalar.activation(pt[1][c][:, s * CH : (s + 1) * CH], acc[:], FUNC.Copy)
+                for a in range(2):
+                    acc = banks.tile([P, CH], F32, name="acc")
+                    for k in range(EB):
+                        nc.tensor.matmul(
+                            acc[:],
+                            w_blocks[a * EB + k][:, c * P : (c + 1) * P],
+                            r[k][s][:],
+                            start=(k == 0),
+                            stop=(k == EB - 1),
+                        )
+                    nc.scalar.activation(pt[a][c][:, s * CH : (s + 1) * CH], acc[:], FUNC.Copy)
 
-        h1 = [[held.tile([P, CH], BF16, name=f"h1_{g}_{e}") for e in range(EB)] for g in range(H1 // CH)]
-        h2 = [[held.tile([P, CH], BF16, name=f"h2_{g}_{e}") for e in range(EB)] for g in range(H2 // CH)]
-        h3 = [[held.tile([P, CH], BF16, name=f"h3_{g}_{e}") for e in range(EB)] for g in range(H3 // CH)]
-
-        def look_up(g, c):
+        def look_up(g, c, h1_block):
             first = g * CH // 16
             left_entries = offsets[:, first : first + CH // 16]
             right_entries = offsets[:, H1 // 16 + first : H1 // 16 + first + CH // 16]
-            u = left_sums.tile([P, CH], F32, name="u")
+            u = sums.tile([P, CH], F32, name="u")
             nc.vector.tensor_tensor(u[:], pt[0][c][:].indirect(left_entries), wb_wide[c][:], ADD)
-            pair = pair_sums.tile([P, CH], F32, name="pair")
-            nc.vector.tensor_tensor(pair[:], pt[1][c][:].indirect(right_entries), u[:], ADD)
-            nc.scalar.activation(h1[g][c][:], pair[:], FUNC.Relu)
+            both = sums.tile([P, CH], F32, name="both")
+            nc.vector.tensor_tensor(both[:], pt[1][c][:].indirect(right_entries), u[:], ADD)
+            nc.vector.tensor_scalar_max(h1_block[:], both[:], 0.0)
 
-        def combine(left, right, parent):
-            accs = [banks.tile([P, CH], F32, name="acc") for c in range(EB)]
+        def combine(families):
+            accs = [[banks.tile([P, CH], F32, name="acc") for c in range(EB)] for family in families]
             for e in range(EB):
-                for side, child in enumerate((left[e], right[e])):
-                    for c in range(EB):
-                        nc.tensor.matmul(
-                            accs[c][:],
-                            w_blocks[side * EB + e][:, c * P : (c + 1) * P],
-                            child[:],
-                            start=(e == 0 and side == 0),
-                            stop=(e == EB - 1 and side == 1),
-                        )
-            for c in range(EB):
-                nc.scalar.activation(parent[c][:], accs[c][:], FUNC.Relu, bias=wb[c][:])
+                for (left, right, parent), family_accs in zip(families, accs):
+                    for side, child in enumerate((left[e], right[e])):
+                        for c in range(EB):
+                            nc.tensor.matmul(
+                                family_accs[c][:],
+                                w_blocks[side * EB + e][:, c * P : (c + 1) * P],
+                                child[:],
+                                start=(e == 0 and side == 0),
+                                stop=(e == EB - 1 and side == 1),
+                            )
+            for (left, right, parent), family_accs in zip(families, accs):
+                for c in range(EB):
+                    nc.scalar.activation(parent[c][:], family_accs[c][:], FUNC.Relu, bias=wb[c][:])
 
         def classify(nodes, first_column):
             for m in range(MB):
@@ -132,15 +114,20 @@ def tile_recursivenn_b_kernel(tc, table, w, w_b, p_w, p_b, offs, out):
                 nc.scalar.activation(scores[:], acc[:], FUNC.Identity, bias=pb[m][:])
                 nc.sync.dma_start(out[m * P : (m + 1) * P, first_column : first_column + CH], scores[:])
 
-        for t in range(H3 // CH):
-            for q in (t, t + H3 // CH):
-                for c in range(EB):
-                    look_up(q, c)
-                    look_up(q + H2 // CH, c)
-                combine(h1[q], h1[q + H2 // CH], h2[q])
-                classify(h1[q], q * CH)
-                classify(h1[q + H2 // CH], (q + H2 // CH) * CH)
-            combine(h2[t], h2[t + H3 // CH], h3[t])
-            classify(h2[t], H1 + t * CH)
-            classify(h2[t + H3 // CH], H1 + (t + H3 // CH) * CH)
-            classify(h3[t], H1 + H2 + t * CH)
+        for t in range(G3):
+            h2_chunks = (t, t + G3)
+            h1_chunks = (t, t + G2, t + G3, t + G3 + G2)
+            h1 = {g: [held.tile([P, CH], BF16, name=f"h1_{i}_{e}") for e in range(EB)] for i, g in enumerate(h1_chunks)}
+            h2 = {q: [held.tile([P, CH], BF16, name=f"h2_{i}_{e}") for e in range(EB)] for i, q in enumerate(h2_chunks)}
+            h3 = [held.tile([P, CH], BF16, name=f"h3_{e}") for e in range(EB)]
+
+            for c in range(EB):
+                for g in h1_chunks:
+                    look_up(g, c, h1[g][c])
+            combine([(h1[q], h1[q + G2], h2[q]) for q in h2_chunks])
+            for g in h1_chunks:
+                classify(h1[g], g * CH)
+            combine([(h2[t], h2[t + G3], h3)])
+            for q in h2_chunks:
+                classify(h2[q], H1 + q * CH)
+            classify(h3, H1 + H2 + t * CH)

@@ -121,12 +121,16 @@ def tile_recursivenn_b_kernel(tc, table, w, w_b, p_w, p_b, offs, out):
             h2 = {q: [held.tile([P, CH], BF16, name=f"h2_{i}_{e}") for e in range(EB)] for i, q in enumerate(h2_chunks)}
             h3 = [held.tile([P, CH], BF16, name=f"h3_{e}") for e in range(EB)]
 
-            for c in range(EB):
-                for g in h1_chunks:
-                    look_up(g, c, h1[g][c])
-            combine([(h1[q], h1[q + G2], h2[q]) for q in h2_chunks])
-            for g in h1_chunks:
-                classify(h1[g], g * CH)
+            groups = [h2_chunks] if t == 0 else [(q,) for q in h2_chunks]
+            for group in groups:
+                for c in range(EB):
+                    for q in group:
+                        look_up(q, c, h1[q][c])
+                        look_up(q + G2, c, h1[q + G2][c])
+                combine([(h1[q], h1[q + G2], h2[q]) for q in group])
+                for q in group:
+                    classify(h1[q], q * CH)
+                    classify(h1[q + G2], (q + G2) * CH)
             combine([(h2[t], h2[t + G3], h3)])
             for q in h2_chunks:
                 classify(h2[q], H1 + q * CH)

@@ -16,7 +16,8 @@ EB = E // P
 MB = M // P
 SB = S // CH
 H1, H2, H3 = N // 2, N // 4, N // 8
-G1, G2, G3 = H1 // CH, H2 // CH, H3 // CH
+G2, G3 = H2 // CH, H3 // CH
+TOGETHER = EB // 2
 
 FLOPS = 2 * (2 * E * E * (S + H2 + H3) + E * M * (H1 + H2 + H3))
 
@@ -72,7 +73,9 @@ def tile_recursivenn_b_kernel(tc, table, w, w_b, p_w, p_b, offs, out):
                         )
                     nc.scalar.activation(pt[a][c][:, s * CH : (s + 1) * CH], acc[:], FUNC.Copy)
 
-        def look_up(g, c, h1_block):
+        h1, h2, h3, h2_banks = {}, {}, {}, {}
+
+        def look_up(g, c):
             first = g * CH // 16
             left_entries = offsets[:, first : first + CH // 16]
             right_entries = offsets[:, H1 // 16 + first : H1 // 16 + first + CH // 16]
@@ -80,24 +83,25 @@ def tile_recursivenn_b_kernel(tc, table, w, w_b, p_w, p_b, offs, out):
             nc.vector.tensor_tensor(u[:], pt[0][c][:].indirect(left_entries), wb_wide[c][:], ADD)
             both = sums.tile([P, CH], F32, name="both")
             nc.vector.tensor_tensor(both[:], pt[1][c][:].indirect(right_entries), u[:], ADD)
-            nc.vector.tensor_scalar_max(h1_block[:], both[:], 0.0)
+            nc.vector.tensor_scalar_max(h1[g][c][:], both[:], 0.0)
 
-        def combine(families):
-            accs = [[banks.tile([P, CH], F32, name="acc") for c in range(EB)] for family in families]
-            for e in range(EB):
-                for (left, right, parent), family_accs in zip(families, accs):
-                    for side, child in enumerate((left[e], right[e])):
-                        for c in range(EB):
-                            nc.tensor.matmul(
-                                family_accs[c][:],
-                                w_blocks[side * EB + e][:, c * P : (c + 1) * P],
-                                child[:],
-                                start=(e == 0 and side == 0),
-                                stop=(e == EB - 1 and side == 1),
-                            )
-            for (left, right, parent), family_accs in zip(families, accs):
+        def open_banks():
+            return [banks.tile([P, CH], F32, name="acc") for c in range(EB)]
+
+        def add_children(accs, left, right, e):
+            for side, child in enumerate((left[e], right[e])):
                 for c in range(EB):
-                    nc.scalar.activation(parent[c][:], family_accs[c][:], FUNC.Relu, bias=wb[c][:])
+                    nc.tensor.matmul(
+                        accs[c][:],
+                        w_blocks[side * EB + e][:, c * P : (c + 1) * P],
+                        child[:],
+                        start=(e == 0 and side == 0),
+                        stop=(e == EB - 1 and side == 1),
+                    )
+
+        def finish_parent(accs, parent):
+            for c in range(EB):
+                nc.scalar.activation(parent[c][:], accs[c][:], FUNC.Relu, bias=wb[c][:])
 
         def classify(nodes, first_column):
             for m in range(MB):
@@ -114,24 +118,37 @@ def tile_recursivenn_b_kernel(tc, table, w, w_b, p_w, p_b, offs, out):
                 nc.scalar.activation(scores[:], acc[:], FUNC.Identity, bias=pb[m][:])
                 nc.sync.dma_start(out[m * P : (m + 1) * P, first_column : first_column + CH], scores[:])
 
+        def leaves_to_h2(q, blocks):
+            for c in blocks:
+                look_up(q, c)
+                look_up(q + G2, c)
+            for e in blocks:
+                if e == 0:
+                    h2_banks[q] = open_banks()
+                add_children(h2_banks[q], h1[q], h1[q + G2], e)
+
         for t in range(G3):
             h2_chunks = (t, t + G3)
-            h1_chunks = (t, t + G2, t + G3, t + G3 + G2)
-            h1 = {g: [held.tile([P, CH], BF16, name=f"h1_{i}_{e}") for e in range(EB)] for i, g in enumerate(h1_chunks)}
-            h2 = {q: [held.tile([P, CH], BF16, name=f"h2_{i}_{e}") for e in range(EB)] for i, q in enumerate(h2_chunks)}
-            h3 = [held.tile([P, CH], BF16, name=f"h3_{e}") for e in range(EB)]
+            for i, g in enumerate((t, t + G2, t + G3, t + G3 + G2)):
+                h1[g] = [held.tile([P, CH], BF16, name=f"h1_{i}_{e}") for e in range(EB)]
+            for i, q in enumerate(h2_chunks):
+                h2[q] = [held.tile([P, CH], BF16, name=f"h2_{i}_{e}") for e in range(EB)]
+            h3[t] = [held.tile([P, CH], BF16, name=f"h3_{e}") for e in range(EB)]
 
-            groups = [h2_chunks] if t == 0 else [(q,) for q in h2_chunks]
-            for group in groups:
-                for c in range(EB):
-                    for q in group:
-                        look_up(q, c, h1[q][c])
-                        look_up(q + G2, c, h1[q + G2][c])
-                combine([(h1[q], h1[q + G2], h2[q]) for q in group])
-                for q in group:
-                    classify(h1[q], q * CH)
-                    classify(h1[q + G2], (q + G2) * CH)
-            combine([(h2[t], h2[t + G3], h3)])
+            together = TOGETHER if t == 0 else 0
+            for c in range(together):
+                for q in h2_chunks:
+                    leaves_to_h2(q, [c])
+            for q in h2_chunks:
+                leaves_to_h2(q, range(together, EB))
+                finish_parent(h2_banks[q], h2[q])
+                classify(h1[q], q * CH)
+                classify(h1[q + G2], (q + G2) * CH)
+
+            h3_banks = open_banks()
+            for e in range(EB):
+                add_children(h3_banks, h2[t], h2[t + G3], e)
+            finish_parent(h3_banks, h3[t])
             for q in h2_chunks:
                 classify(h2[q], H1 + q * CH)
-            classify(h3, H1 + H2 + t * CH)
+            classify(h3[t], H1 + H2 + t * CH)

@@ -144,11 +144,12 @@ def tile_recursivenn_b_kernel(tc, table, w, w_b, p_w, p_b, offs, out):
                 finish_parent(h2_banks[q], h2[q])
                 classify(h1[q], q * CH)
                 classify(h1[q + G2], (q + G2) * CH)
+                if q == t:
+                    classify(h2[t], H1 + t * CH)
 
             h3_banks = open_banks()
             for e in range(EB):
                 add_children(h3_banks, h2[t], h2[t + G3], e)
             finish_parent(h3_banks, h3[t])
-            for q in h2_chunks:
-                classify(h2[q], H1 + q * CH)
+            classify(h2[t + G3], H1 + (t + G3) * CH)
             classify(h3[t], H1 + H2 + t * CH)

@@ -31,9 +31,14 @@ def tile_recursivenn_b_kernel(tc, table, w, w_b, p_w, p_b, offs, out):
         tc.tile_pool(name="results", bufs=6) as results,
         tc.psum_pool(name="banks", bufs=8) as banks,
     ):
-        w_blocks = [held.tile([P, E], BF16, name=f"w{k}") for k in range(2 * EB)]
-        for k in range(2 * EB):
-            nc.scalar.dma_start(w_blocks[k][:], w[k * P : (k + 1) * P, :])
+        w_by_block = w.rearrange("(a k p) c -> k p a c", a=2, k=EB, p=P)
+        w_pairs = [held.tile([P, 2, E], BF16, name=f"w_pair{k}") for k in range(EB)]
+        for k in range(EB):
+            nc.scalar.dma_start(w_pairs[k][:], w_by_block[k])
+        wb = held.tile([P, EB], F32, name="wb")
+        nc.scalar.dma_start(wb[:], w_b.rearrange("(c p) o -> p (c o)", p=P))
+        pb = held.tile([P, MB], F32, name="pb")
+        nc.scalar.dma_start(pb[:], p_b.rearrange("(m p) o -> p (m o)", p=P))
 
         r = [[held.tile([P, CH], BF16, name=f"r{k}_{s}") for s in range(SB)] for k in range(EB)]
         for s in range(SB):
@@ -48,30 +53,30 @@ def tile_recursivenn_b_kernel(tc, table, w, w_b, p_w, p_b, offs, out):
         for k in range(EB):
             nc.sync.dma_start(pw_blocks[k][:], p_w[k * P : (k + 1) * P, :])
 
-        wb = [held.tile([P, 1], F32, name=f"wb{c}") for c in range(EB)]
-        for c in range(EB):
-            nc.scalar.dma_start(wb[c][:], w_b[c * P : (c + 1) * P, :])
-        pb = [held.tile([P, 1], F32, name=f"pb{m}") for m in range(MB)]
-        for m in range(MB):
-            nc.scalar.dma_start(pb[m][:], p_b[m * P : (m + 1) * P, :])
         wb_wide = [held.tile([P, CH], F32, name=f"wb_wide{c}") for c in range(EB)]
         for c in range(EB):
-            nc.vector.tensor_copy(wb_wide[c][:], wb[c][:].to_broadcast([P, CH]))
+            nc.vector.tensor_copy(wb_wide[c][:], wb[:, c : c + 1].to_broadcast([P, CH]))
 
         pt = [[held.tile([P, S], F32, name=f"pt{a}_{c}") for c in range(EB)] for a in range(2)]
+
+        def project(blocks, s):
+            accs = {(c, a): banks.tile([P, CH], F32, name="acc") for c in blocks for a in range(2)}
+            for k in range(EB):
+                for c, a in accs:
+                    nc.tensor.matmul(
+                        accs[c, a][:],
+                        w_pairs[k][:, a, c * P : (c + 1) * P],
+                        r[k][s][:],
+                        start=(k == 0),
+                        stop=(k == EB - 1),
+                    )
+            for c, a in accs:
+                nc.scalar.activation(pt[a][c][:, s * CH : (s + 1) * CH], accs[c, a][:], FUNC.Copy)
+
+        project((0, 1), 0)
         for c in range(EB):
-            for s in range(SB):
-                for a in range(2):
-                    acc = banks.tile([P, CH], F32, name="acc")
-                    for k in range(EB):
-                        nc.tensor.matmul(
-                            acc[:],
-                            w_blocks[a * EB + k][:, c * P : (c + 1) * P],
-                            r[k][s][:],
-                            start=(k == 0),
-                            stop=(k == EB - 1),
-                        )
-                    nc.scalar.activation(pt[a][c][:, s * CH : (s + 1) * CH], acc[:], FUNC.Copy)
+            for s in range(1 if c < 2 else 0, SB):
+                project((c,), s)
 
         h1, h2, h3, h2_banks = {}, {}, {}, {}
 
@@ -93,7 +98,7 @@ def tile_recursivenn_b_kernel(tc, table, w, w_b, p_w, p_b, offs, out):
                 for c in range(EB):
                     nc.tensor.matmul(
                         accs[c][:],
-                        w_blocks[side * EB + e][:, c * P : (c + 1) * P],
+                        w_pairs[e][:, side, c * P : (c + 1) * P],
                         child[:],
                         start=(e == 0 and side == 0),
                         stop=(e == EB - 1 and side == 1),
@@ -101,22 +106,26 @@ def tile_recursivenn_b_kernel(tc, table, w, w_b, p_w, p_b, offs, out):
 
         def finish_parent(accs, parent):
             for c in range(EB):
-                nc.scalar.activation(parent[c][:], accs[c][:], FUNC.Relu, bias=wb[c][:])
+                nc.scalar.activation(parent[c][:], accs[c][:], FUNC.Relu, bias=wb[:, c : c + 1])
 
-        def classify(nodes, first_column):
+        def classify(nodes, first_column, pieces=1):
+            width = CH // pieces
             for m in range(MB):
-                acc = banks.tile([P, CH], F32, name="acc")
-                for e in range(EB):
-                    nc.tensor.matmul(
-                        acc[:],
-                        pw_blocks[e][:, m * P : (m + 1) * P],
-                        nodes[e][:],
-                        start=(e == 0),
-                        stop=(e == EB - 1),
+                for lo in range(0, CH, width):
+                    acc = banks.tile([P, width], F32, name="acc")
+                    for e in range(EB):
+                        nc.tensor.matmul(
+                            acc[:],
+                            pw_blocks[e][:, m * P : (m + 1) * P],
+                            nodes[e][:, lo : lo + width],
+                            start=(e == 0),
+                            stop=(e == EB - 1),
+                        )
+                    scores = results.tile([P, width], F32, name="scores")
+                    nc.scalar.activation(scores[:], acc[:], FUNC.Identity, bias=pb[:, m : m + 1])
+                    nc.sync.dma_start(
+                        out[m * P : (m + 1) * P, first_column + lo : first_column + lo + width], scores[:]
                     )
-                scores = results.tile([P, CH], F32, name="scores")
-                nc.scalar.activation(scores[:], acc[:], FUNC.Identity, bias=pb[m][:])
-                nc.sync.dma_start(out[m * P : (m + 1) * P, first_column : first_column + CH], scores[:])
 
         def leaves_to_h2(q, blocks):
             for c in blocks:
@@ -152,4 +161,4 @@ def tile_recursivenn_b_kernel(tc, table, w, w_b, p_w, p_b, offs, out):
                 add_children(h3_banks, h2[t], h2[t + G3], e)
             finish_parent(h3_banks, h3[t])
             classify(h2[t + G3], H1 + (t + G3) * CH)
-            classify(h3[t], H1 + H2 + t * CH)
+            classify(h3[t], H1 + H2 + t * CH, pieces=(2 if t == G3 - 1 else 1))

@@ -93,16 +93,24 @@ def tile_recursivenn_b_kernel(tc, table, w, w_b, p_w, p_b, offs, out):
         def open_banks():
             return [banks.tile([P, CH], F32, name="acc") for c in range(EB)]
 
+        def add(accs, c, side, child, e):
+            nc.tensor.matmul(
+                accs[c][:],
+                w_pairs[e][:, side, c * P : (c + 1) * P],
+                child[e][:],
+                start=(side == 0 and e == 0),
+                stop=(side == 1 and e == EB - 1),
+            )
+
         def add_children(accs, left, right, e):
-            for side, child in enumerate((left[e], right[e])):
+            if e < EB - 1:
+                for side, child in enumerate((left, right)):
+                    for c in range(EB):
+                        add(accs, c, side, child, e)
+            else:
                 for c in range(EB):
-                    nc.tensor.matmul(
-                        accs[c][:],
-                        w_pairs[e][:, side, c * P : (c + 1) * P],
-                        child[:],
-                        start=(e == 0 and side == 0),
-                        stop=(e == EB - 1 and side == 1),
-                    )
+                    for side, child in enumerate((left, right)):
+                        add(accs, c, side, child, e)
 
         def finish_parent(accs, parent):
             for c in range(EB):
@@ -155,10 +163,14 @@ def tile_recursivenn_b_kernel(tc, table, w, w_b, p_w, p_b, offs, out):
                 classify(h1[q + G2], (q + G2) * CH)
                 if q == t:
                     classify(h2[t], H1 + t * CH)
+                    h3_banks = open_banks()
+                    for e in range(EB):
+                        for c in range(EB):
+                            add(h3_banks, c, 0, h2[t], e)
 
-            h3_banks = open_banks()
             for e in range(EB):
-                add_children(h3_banks, h2[t], h2[t + G3], e)
+                for c in range(EB):
+                    add(h3_banks, c, 1, h2[t + G3], e)
             finish_parent(h3_banks, h3[t])
             classify(h2[t + G3], H1 + (t + G3) * CH)
             classify(h3[t], H1 + H2 + t * CH, pieces=(2 if t == G3 - 1 else 1))

@@ -36,9 +36,7 @@ def tile_recursivenn_b_kernel(tc, table, w, w_b, p_w, p_b, offs, out):
         for k in range(EB):
             nc.scalar.dma_start(w_pairs[k][:], w_by_block[k])
         wb = held.tile([P, EB], F32, name="wb")
-        nc.scalar.dma_start(wb[:], w_b.rearrange("(c p) o -> p (c o)", p=P))
         pb = held.tile([P, MB], F32, name="pb")
-        nc.scalar.dma_start(pb[:], p_b.rearrange("(m p) o -> p (m o)", p=P))
 
         r = [[held.tile([P, CH], BF16, name=f"r{k}_{s}") for s in range(SB)] for k in range(EB)]
         for s in range(SB):
@@ -46,12 +44,15 @@ def tile_recursivenn_b_kernel(tc, table, w, w_b, p_w, p_b, offs, out):
                 raw = loaded.tile([P, CH], F32, name="raw")
                 nc.sync.dma_start(raw[:], table[k * P : (k + 1) * P, s * CH : (s + 1) * CH])
                 nc.vector.tensor_scalar_max(r[k][s][:], raw[:], 0.0)
+            if s == 1:
+                nc.sync.dma_start(wb[:], w_b.rearrange("(c p) o -> p (c o)", p=P))
 
         offsets = held.tile([P, N // 16], U16, name="offsets")
         nc.sync.dma_start(offsets[:], offs)
         pw_blocks = [held.tile([P, M], BF16, name=f"pw{k}") for k in range(EB)]
         for k in range(EB):
             nc.sync.dma_start(pw_blocks[k][:], p_w[k * P : (k + 1) * P, :])
+        nc.sync.dma_start(pb[:], p_b.rearrange("(m p) o -> p (m o)", p=P))
 
         wb_wide = [held.tile([P, CH], F32, name=f"wb_wide{c}") for c in range(EB)]
         for c in range(EB):

@@ -74,9 +74,10 @@ def tile_recursivenn_b_kernel(tc, table, w, w_b, p_w, p_b, offs, out):
             for c, a in accs:
                 nc.scalar.activation(pt[a][c][:, s * CH : (s + 1) * CH], accs[c, a][:], FUNC.Copy)
 
-        project((0, 1), 0)
+        for s in range(2):
+            project((0, 1), s)
         for c in range(EB):
-            for s in range(1 if c < 2 else 0, SB):
+            for s in range(2 if c < 2 else 0, SB):
                 project((c,), s)
 
         h1, h2, h3, h2_banks = {}, {}, {}, {}

@@ -44,11 +44,10 @@ def tile_recursivenn_b_kernel(tc, table, w, w_b, p_w, p_b, offs, out):
                 raw = loaded.tile([P, CH], F32, name="raw")
                 nc.sync.dma_start(raw[:], table[k * P : (k + 1) * P, s * CH : (s + 1) * CH])
                 nc.vector.tensor_scalar_max(r[k][s][:], raw[:], 0.0)
-            if s == 1:
-                nc.sync.dma_start(wb[:], w_b.rearrange("(c p) o -> p (c o)", p=P))
 
         offsets = held.tile([P, N // 16], U16, name="offsets")
         nc.sync.dma_start(offsets[:], offs)
+        nc.sync.dma_start(wb[:], w_b.rearrange("(c p) o -> p (c o)", p=P))
         pw_blocks = [held.tile([P, M], BF16, name=f"pw{k}") for k in range(EB)]
         for k in range(EB):
             nc.sync.dma_start(pw_blocks[k][:], p_w[k * P : (k + 1) * P, :])

@@ -15,6 +15,7 @@ CH = 512
 EB = E // P
 MB = M // P
 SB = S // CH
+PIECES = [(0, CH // 2), (CH // 2, CH // 2)] + [(s * CH, CH) for s in range(1, SB)]
 H1, H2, H3 = N // 2, N // 4, N // 8
 G2, G3 = H2 // CH, H3 // CH
 TOGETHER = EB // 2
@@ -26,7 +27,7 @@ def tile_recursivenn_b_kernel(tc, table, w, w_b, p_w, p_b, offs, out):
     nc = tc.nc
     with (
         tc.tile_pool(name="held", bufs=1) as held,
-        tc.tile_pool(name="loaded", bufs=SB * EB) as loaded,
+        tc.tile_pool(name="loaded", bufs=len(PIECES) * EB) as loaded,
         tc.tile_pool(name="sums", bufs=3) as sums,
         tc.tile_pool(name="results", bufs=6) as results,
         tc.psum_pool(name="banks", bufs=8) as banks,
@@ -38,12 +39,12 @@ def tile_recursivenn_b_kernel(tc, table, w, w_b, p_w, p_b, offs, out):
         wb = held.tile([P, EB], F32, name="wb")
         pb = held.tile([P, MB], F32, name="pb")
 
-        r = [[held.tile([P, CH], BF16, name=f"r{k}_{s}") for s in range(SB)] for k in range(EB)]
-        for s in range(SB):
+        r = [[held.tile([P, words], BF16, name=f"r{k}_{i}") for i, (lo, words) in enumerate(PIECES)] for k in range(EB)]
+        for i, (lo, words) in enumerate(PIECES):
             for k in range(EB):
-                raw = loaded.tile([P, CH], F32, name="raw")
-                nc.sync.dma_start(raw[:], table[k * P : (k + 1) * P, s * CH : (s + 1) * CH])
-                nc.vector.tensor_scalar_max(r[k][s][:], raw[:], 0.0)
+                raw = loaded.tile([P, words], F32, name="raw")
+                nc.sync.dma_start(raw[:], table[k * P : (k + 1) * P, lo : lo + words])
+                nc.vector.tensor_scalar_max(r[k][i][:], raw[:], 0.0)
 
         offsets = held.tile([P, N // 16], U16, name="offsets")
         nc.sync.dma_start(offsets[:], offs)
@@ -59,25 +60,27 @@ def tile_recursivenn_b_kernel(tc, table, w, w_b, p_w, p_b, offs, out):
 
         pt = [[held.tile([P, S], F32, name=f"pt{a}_{c}") for c in range(EB)] for a in range(2)]
 
-        def project(blocks, s):
-            accs = {(c, a): banks.tile([P, CH], F32, name="acc") for c in blocks for a in range(2)}
+        def project(blocks, i):
+            lo, words = PIECES[i]
+            accs = {(c, a): banks.tile([P, words], F32, name="acc") for c in blocks for a in range(2)}
             for k in range(EB):
                 for c, a in accs:
                     nc.tensor.matmul(
                         accs[c, a][:],
                         w_pairs[k][:, a, c * P : (c + 1) * P],
-                        r[k][s][:],
+                        r[k][i][:],
                         start=(k == 0),
                         stop=(k == EB - 1),
                     )
             for c, a in accs:
-                nc.scalar.activation(pt[a][c][:, s * CH : (s + 1) * CH], accs[c, a][:], FUNC.Copy)
+                nc.scalar.activation(pt[a][c][:, lo : lo + words], accs[c, a][:], FUNC.Copy)
 
-        for s in range(2):
-            project((0, 1), s)
+        DOUBLE = len(PIECES) - SB // 2
+        for i in range(DOUBLE):
+            project((0, 1), i)
         for c in range(EB):
-            for s in range(2 if c < 2 else 0, SB):
-                project((c,), s)
+            for i in range(DOUBLE if c < 2 else 0, len(PIECES)):
+                project((c,), i)
 
         h1, h2, h3, h2_banks = {}, {}, {}, {}
 

@@ -18,7 +18,7 @@ SB = S // CH
 PIECES = [(0, CH // 2), (CH // 2, CH // 2)] + [(s * CH, CH) for s in range(1, SB)]
 H1, H2, H3 = N // 2, N // 4, N // 8
 G2, G3 = H2 // CH, H3 // CH
-TOGETHER = EB // 2
+TOGETHER = 1
 
 FLOPS = 2 * (2 * E * E * (S + H2 + H3) + E * M * (H1 + H2 + H3))
 

@@ -76,10 +76,12 @@ def tile_recursivenn_b_kernel(tc, table, w, w_b, p_w, p_b, offs, out):
                 nc.scalar.activation(pt[a][c][:, lo : lo + words], accs[c, a][:], FUNC.Copy)
 
         DOUBLE = len(PIECES) - SB // 2
-        for i in range(DOUBLE):
+        FIRST = 3
+        project(range(FIRST), 0)
+        for i in range(1, DOUBLE):
             project((0, 1), i)
         for c in range(EB):
-            for i in range(DOUBLE if c < 2 else 0, len(PIECES)):
+            for i in range(DOUBLE if c < 2 else 1 if c < FIRST else 0, len(PIECES)):
                 project((c,), i)
 
         h1, h2, h3, h2_banks = {}, {}, {}, {}

@@ -34,7 +34,8 @@ def tile_recursivenn_b_kernel(tc, table, w, w_b, p_w, p_b, offs, out):
     ):
         w_by_block = w.rearrange("(a k p) c -> k p a c", a=2, k=EB, p=P)
         w_pairs = [held.tile([P, 2, E], BF16, name=f"w_pair{k}") for k in range(EB)]
-        for k in range(EB):
+        nc.scalar.dma_start(w_pairs[0][:, 0, :], w_by_block[0][:, 0, :])
+        for k in range(1, EB):
             nc.scalar.dma_start(w_pairs[k][:], w_by_block[k])
         wb = held.tile([P, EB], F32, name="wb")
         pb = held.tile([P, MB], F32, name="pb")
@@ -44,6 +45,8 @@ def tile_recursivenn_b_kernel(tc, table, w, w_b, p_w, p_b, offs, out):
             for k in range(EB):
                 raw = loaded.tile([P, words], F32, name="raw")
                 nc.sync.dma_start(raw[:], table[k * P : (k + 1) * P, lo : lo + words])
+                if (i, k) == (0, 0):
+                    nc.sync.dma_start(w_pairs[0][:, 1, :], w_by_block[0][:, 1, :])
                 nc.vector.tensor_scalar_max(r[k][i][:], raw[:], 0.0)
 
         offsets = held.tile([P, N // 16], U16, name="offsets")
@@ -62,7 +65,7 @@ def tile_recursivenn_b_kernel(tc, table, w, w_b, p_w, p_b, offs, out):
 
         def project(blocks, i):
             lo, words = PIECES[i]
-            accs = {(c, a): banks.tile([P, words], F32, name="acc") for c in blocks for a in range(2)}
+            accs = {(c, a): banks.tile([P, words], F32, name="acc") for a in range(2) for c in blocks}
             for k in range(EB):
                 for c, a in accs:
                     nc.tensor.matmul(

@@ -15,7 +15,7 @@ CH = 512
 EB = E // P
 MB = M // P
 SB = S // CH
-PIECES = [(0, CH // 2), (CH // 2, CH // 2)] + [(s * CH, CH) for s in range(1, SB)]
+PIECES = [(0, CH // 4), (CH // 4, CH - CH // 4)] + [(s * CH, CH) for s in range(1, SB)]
 H1, H2, H3 = N // 2, N // 4, N // 8
 G2, G3 = H2 // CH, H3 // CH
 TOGETHER = 1
@@ -34,7 +34,8 @@ def tile_recursivenn_b_kernel(tc, table, w, w_b, p_w, p_b, offs, out):
     ):
         w_by_block = w.rearrange("(a k p) c -> k p a c", a=2, k=EB, p=P)
         w_pairs = [held.tile([P, 2, E], BF16, name=f"w_pair{k}") for k in range(EB)]
-        nc.scalar.dma_start(w_pairs[0][:, 0, :], w_by_block[0][:, 0, :])
+        for half in (slice(0, E // 2), slice(E // 2, E)):
+            nc.scalar.dma_start(w_pairs[0][:, 0, half], w_by_block[0][:, 0, half])
         for k in range(1, EB):
             nc.scalar.dma_start(w_pairs[k][:], w_by_block[k])
         wb = held.tile([P, EB], F32, name="wb")
@@ -79,7 +80,7 @@ def tile_recursivenn_b_kernel(tc, table, w, w_b, p_w, p_b, offs, out):
                 nc.scalar.activation(pt[a][c][:, lo : lo + words], accs[c, a][:], FUNC.Copy)
 
         DOUBLE = len(PIECES) - SB // 2
-        FIRST = 3
+        FIRST = 4
         project(range(FIRST), 0)
         for i in range(1, DOUBLE):
             project((0, 1), i)

@@ -15,7 +15,7 @@ CH = 512
 EB = E // P
 MB = M // P
 SB = S // CH
-PIECES = [(0, CH // 4), (CH // 4, CH - CH // 4)] + [(s * CH, CH) for s in range(1, SB)]
+PIECES = [(0, CH // 2), (CH // 2, CH // 2)] + [(s * CH, CH) for s in range(1, SB)]
 H1, H2, H3 = N // 2, N // 4, N // 8
 G2, G3 = H2 // CH, H3 // CH
 TOGETHER = 1
@@ -29,15 +29,18 @@ def tile_recursivenn_b_kernel(tc, table, w, w_b, p_w, p_b, offs, out):
         tc.tile_pool(name="held", bufs=1) as held,
         tc.tile_pool(name="loaded", bufs=len(PIECES) * EB) as loaded,
         tc.tile_pool(name="sums", bufs=3) as sums,
-        tc.tile_pool(name="results", bufs=6) as results,
+        tc.tile_pool(name="results", bufs=8) as results,
         tc.psum_pool(name="banks", bufs=8) as banks,
     ):
-        w_by_block = w.rearrange("(a k p) c -> k p a c", a=2, k=EB, p=P)
-        w_pairs = [held.tile([P, 2, E], BF16, name=f"w_pair{k}") for k in range(EB)]
-        for half in (slice(0, E // 2), slice(E // 2, E)):
-            nc.scalar.dma_start(w_pairs[0][:, 0, half], w_by_block[0][:, 0, half])
+        w_rows = [[held.tile([P, E], BF16, name=f"w{a}_{k}") for k in range(EB)] for a in range(2)]
+
+        def load_w(queue, a, k, columns):
+            queue.dma_start(w_rows[a][k][:, columns], w[(a * EB + k) * P : (a * EB + k + 1) * P, columns])
+
+        load_w(nc.scalar, 0, 0, slice(0, E // 2))
+        load_w(nc.scalar, 0, 0, slice(E // 2, E))
         for k in range(1, EB):
-            nc.scalar.dma_start(w_pairs[k][:], w_by_block[k])
+            load_w(nc.scalar, 0, k, slice(0, E))
         wb = held.tile([P, EB], F32, name="wb")
         pb = held.tile([P, MB], F32, name="pb")
 
@@ -46,16 +49,15 @@ def tile_recursivenn_b_kernel(tc, table, w, w_b, p_w, p_b, offs, out):
             for k in range(EB):
                 raw = loaded.tile([P, words], F32, name="raw")
                 nc.sync.dma_start(raw[:], table[k * P : (k + 1) * P, lo : lo + words])
-                if (i, k) == (0, 0):
-                    nc.sync.dma_start(w_pairs[0][:, 1, :], w_by_block[0][:, 1, :])
                 nc.vector.tensor_scalar_max(r[k][i][:], raw[:], 0.0)
+                if i == 0:
+                    load_w(nc.sync, 1, k, slice(0, E))
 
         offsets = held.tile([P, N // 16], U16, name="offsets")
         nc.sync.dma_start(offsets[:], offs)
         nc.sync.dma_start(wb[:], w_b.rearrange("(c p) o -> p (c o)", p=P))
-        pw_blocks = [held.tile([P, M], BF16, name=f"pw{k}") for k in range(EB)]
-        for k in range(EB):
-            nc.sync.dma_start(pw_blocks[k][:], p_w[k * P : (k + 1) * P, :])
+        pw_blocks = held.tile([P, EB, M], BF16, name="pw_blocks")
+        nc.sync.dma_start(pw_blocks[:], p_w.rearrange("(k p) m -> p k m", p=P))
         nc.sync.dma_start(pb[:], p_b.rearrange("(m p) o -> p (m o)", p=P))
 
         wb_wide = [held.tile([P, CH], F32, name=f"wb_wide{c}") for c in range(EB)]
@@ -71,7 +73,7 @@ def tile_recursivenn_b_kernel(tc, table, w, w_b, p_w, p_b, offs, out):
                 for c, a in accs:
                     nc.tensor.matmul(
                         accs[c, a][:],
-                        w_pairs[k][:, a, c * P : (c + 1) * P],
+                        w_rows[a][k][:, c * P : (c + 1) * P],
                         r[k][i][:],
                         start=(k == 0),
                         stop=(k == EB - 1),
@@ -106,7 +108,7 @@ def tile_recursivenn_b_kernel(tc, table, w, w_b, p_w, p_b, offs, out):
         def add(accs, c, side, child, e):
             nc.tensor.matmul(
                 accs[c][:],
-                w_pairs[e][:, side, c * P : (c + 1) * P],
+                w_rows[side][e][:, c * P : (c + 1) * P],
                 child[e][:],
                 start=(side == 0 and e == 0),
                 stop=(side == 1 and e == EB - 1),
@@ -126,24 +128,30 @@ def tile_recursivenn_b_kernel(tc, table, w, w_b, p_w, p_b, offs, out):
             for c in range(EB):
                 nc.scalar.activation(parent[c][:], accs[c][:], FUNC.Relu, bias=wb[:, c : c + 1])
 
-        def classify(nodes, first_column, pieces=1):
-            width = CH // pieces
-            for m in range(MB):
-                for lo in range(0, CH, width):
-                    acc = banks.tile([P, width], F32, name="acc")
-                    for e in range(EB):
-                        nc.tensor.matmul(
-                            acc[:],
-                            pw_blocks[e][:, m * P : (m + 1) * P],
-                            nodes[e][:, lo : lo + width],
-                            start=(e == 0),
-                            stop=(e == EB - 1),
-                        )
-                    scores = results.tile([P, width], F32, name="scores")
-                    nc.scalar.activation(scores[:], acc[:], FUNC.Identity, bias=pb[:, m : m + 1])
-                    nc.sync.dma_start(
-                        out[m * P : (m + 1) * P, first_column + lo : first_column + lo + width], scores[:]
+        def classify(nodes, first_column, last=False):
+            parts = [(m, 0, CH) for m in range(MB)]
+            if last:
+                half, quarter = CH // 2, CH // 4
+                parts[-1:] = [(MB - 1, 0, half), (MB - 1, half, quarter), (MB - 1, half + quarter, quarter)]
+            for part, (m, lo, width) in enumerate(parts):
+                acc = banks.tile([P, width], F32, name="acc")
+                for e in range(EB):
+                    nc.tensor.matmul(
+                        acc[:],
+                        pw_blocks[:, e, m * P : (m + 1) * P],
+                        nodes[e][:, lo : lo + width],
+                        start=(e == 0),
+                        stop=(e == EB - 1),
                     )
+                scores = results.tile([P, width], F32, name="scores")
+                if last and part % 2 == 0:
+                    nc.vector.tensor_scalar_add(scores[:], acc[:], pb[:, m : m + 1])
+                else:
+                    nc.scalar.activation(scores[:], acc[:], FUNC.Identity, bias=pb[:, m : m + 1])
+                queue = nc.scalar if last and part == len(parts) - 1 else nc.sync
+                queue.dma_start(
+                    out[m * P : (m + 1) * P, first_column + lo : first_column + lo + width], scores[:]
+                )
 
         def leaves_to_h2(q, blocks):
             for c in blocks:
@@ -183,4 +191,4 @@ def tile_recursivenn_b_kernel(tc, table, w, w_b, p_w, p_b, offs, out):
                     add(h3_banks, c, 1, h2[t + G3], e)
             finish_parent(h3_banks, h3[t])
             classify(h2[t + G3], H1 + (t + G3) * CH)
-            classify(h3[t], H1 + H2 + t * CH, pieces=(2 if t == G3 - 1 else 1))
+            classify(h3[t], H1 + H2 + t * CH, last=(t == G3 - 1))

@@ -132,7 +132,8 @@ def tile_recursivenn_b_kernel(tc, table, w, w_b, p_w, p_b, offs, out):
             parts = [(m, 0, CH) for m in range(MB)]
             if last:
                 half, quarter = CH // 2, CH // 4
-                parts[-1:] = [(MB - 1, 0, half), (MB - 1, half, quarter), (MB - 1, half + quarter, quarter)]
+                parts = [(m, lo, half) for m in range(MB) for lo in (0, half)]
+                parts[-1:] = [(MB - 1, lo, quarter) for lo in (half, half + quarter)]
             for part, (m, lo, width) in enumerate(parts):
                 acc = banks.tile([P, width], F32, name="acc")
                 for e in range(EB):
@@ -144,12 +145,11 @@ def tile_recursivenn_b_kernel(tc, table, w, w_b, p_w, p_b, offs, out):
                         stop=(e == EB - 1),
                     )
                 scores = results.tile([P, width], F32, name="scores")
-                if last and part % 2 == 0:
+                if last and part % 2 == 1:
                     nc.vector.tensor_scalar_add(scores[:], acc[:], pb[:, m : m + 1])
                 else:
                     nc.scalar.activation(scores[:], acc[:], FUNC.Identity, bias=pb[:, m : m + 1])
-                queue = nc.scalar if last and part == len(parts) - 1 else nc.sync
-                queue.dma_start(
+                nc.sync.dma_start(
                     out[m * P : (m + 1) * P, first_column + lo : first_column + lo + width], scores[:]
                 )
 

@@ -34,13 +34,9 @@ def tile_recursivenn_b_kernel(tc, table, w, w_b, p_w, p_b, offs, out):
     ):
         w_rows = [[held.tile([P, E], BF16, name=f"w{a}_{k}") for k in range(EB)] for a in range(2)]
 
-        def load_w(queue, a, k, columns):
-            queue.dma_start(w_rows[a][k][:, columns], w[(a * EB + k) * P : (a * EB + k + 1) * P, columns])
+        def load_w(a, k, columns):
+            nc.sync.dma_start(w_rows[a][k][:, columns], w[(a * EB + k) * P : (a * EB + k + 1) * P, columns])
 
-        load_w(nc.scalar, 0, 0, slice(0, E // 2))
-        load_w(nc.scalar, 0, 0, slice(E // 2, E))
-        for k in range(1, EB):
-            load_w(nc.scalar, 0, k, slice(0, E))
         wb = held.tile([P, EB], F32, name="wb")
         pb = held.tile([P, MB], F32, name="pb")
 
@@ -51,7 +47,9 @@ def tile_recursivenn_b_kernel(tc, table, w, w_b, p_w, p_b, offs, out):
                 nc.sync.dma_start(raw[:], table[k * P : (k + 1) * P, lo : lo + words])
                 nc.vector.tensor_scalar_max(r[k][i][:], raw[:], 0.0)
                 if i == 0:
-                    load_w(nc.sync, 1, k, slice(0, E))
+                    for columns in (slice(0, E // 2), slice(E // 2, E)) if k == 0 else (slice(0, E),):
+                        load_w(0, k, columns)
+                    load_w(1, k, slice(0, E))
 
         offsets = held.tile([P, N // 16], U16, name="offsets")
         nc.sync.dma_start(offsets[:], offs)

import concourse.mybir as mybir

F32 = mybir.dt.float32
BF16 = mybir.dt.bfloat16
U16 = mybir.dt.uint16
ADD = mybir.AluOpType.add
FUNC = mybir.ActivationFunctionType

P = 128
E = 512
S = 2048
N = 8192
M = 256
CH = 512
EB = E // P
MB = M // P
SB = S // CH
PIECES = [(0, CH // 2), (CH // 2, CH // 2)] + [(s * CH, CH) for s in range(1, SB)]
H1, H2, H3 = N // 2, N // 4, N // 8
G2, G3 = H2 // CH, H3 // CH
TOGETHER = 1

FLOPS = 2 * (2 * E * E * (S + H2 + H3) + E * M * (H1 + H2 + H3))


def tile_recursivenn_b_kernel(tc, table, w, w_b, p_w, p_b, offs, out):
    nc = tc.nc
    with (
        tc.tile_pool(name="held", bufs=1) as held,
        tc.tile_pool(name="loaded", bufs=len(PIECES) * EB) as loaded,
        tc.tile_pool(name="sums", bufs=3) as sums,
        tc.tile_pool(name="results", bufs=8) as results,
        tc.psum_pool(name="banks", bufs=8) as banks,
    ):
        w_rows = [[held.tile([P, E], BF16, name=f"w{a}_{k}") for k in range(EB)] for a in range(2)]

        def load_w(a, k, columns):
            nc.sync.dma_start(w_rows[a][k][:, columns], w[(a * EB + k) * P : (a * EB + k + 1) * P, columns])

        wb = held.tile([P, EB], F32, name="wb")
        pb = held.tile([P, MB], F32, name="pb")

        r = [[held.tile([P, words], BF16, name=f"r{k}_{i}") for i, (lo, words) in enumerate(PIECES)] for k in range(EB)]
        for i, (lo, words) in enumerate(PIECES):
            for k in range(EB):
                raw = loaded.tile([P, words], F32, name="raw")
                nc.sync.dma_start(raw[:], table[k * P : (k + 1) * P, lo : lo + words])
                nc.vector.tensor_scalar_max(r[k][i][:], raw[:], 0.0)
                if i == 0:
                    for columns in (slice(0, E // 2), slice(E // 2, E)) if k == 0 else (slice(0, E),):
                        load_w(0, k, columns)
                    load_w(1, k, slice(0, E))

        offsets = held.tile([P, N // 16], U16, name="offsets")
        nc.sync.dma_start(offsets[:], offs)
        nc.sync.dma_start(wb[:], w_b.rearrange("(c p) o -> p (c o)", p=P))
        pw_blocks = held.tile([P, EB, M], BF16, name="pw_blocks")
        nc.sync.dma_start(pw_blocks[:], p_w.rearrange("(k p) m -> p k m", p=P))
        nc.sync.dma_start(pb[:], p_b.rearrange("(m p) o -> p (m o)", p=P))

        wb_wide = [held.tile([P, CH], F32, name=f"wb_wide{c}") for c in range(EB)]
        for c in range(EB):
            nc.vector.tensor_copy(wb_wide[c][:], wb[:, c : c + 1].to_broadcast([P, CH]))

        pt = [[held.tile([P, S], F32, name=f"pt{a}_{c}") for c in range(EB)] for a in range(2)]

        def project(blocks, i):
            lo, words = PIECES[i]
            accs = {(c, a): banks.tile([P, words], F32, name="acc") for a in range(2) for c in blocks}
            for k in range(EB):
                for c, a in accs:
                    nc.tensor.matmul(
                        accs[c, a][:],
                        w_rows[a][k][:, c * P : (c + 1) * P],
                        r[k][i][:],
                        start=(k == 0),
                        stop=(k == EB - 1),
                    )
            for c, a in accs:
                nc.scalar.activation(pt[a][c][:, lo : lo + words], accs[c, a][:], FUNC.Copy)

        DOUBLE = len(PIECES) - SB // 2
        FIRST = 4
        project(range(FIRST), 0)
        for i in range(1, DOUBLE):
            project((0, 1), i)
        for c in range(EB):
            for i in range(DOUBLE if c < 2 else 1 if c < FIRST else 0, len(PIECES)):
                project((c,), i)

        h1, h2, h3, h2_banks = {}, {}, {}, {}

        def look_up(g, c):
            first = g * CH // 16
            left_entries = offsets[:, first : first + CH // 16]
            right_entries = offsets[:, H1 // 16 + first : H1 // 16 + first + CH // 16]
            u = sums.tile([P, CH], F32, name="u")
            nc.vector.tensor_tensor(u[:], pt[0][c][:].indirect(left_entries), wb_wide[c][:], ADD)
            both = sums.tile([P, CH], F32, name="both")
            nc.vector.tensor_tensor(both[:], pt[1][c][:].indirect(right_entries), u[:], ADD)
            nc.vector.tensor_scalar_max(h1[g][c][:], both[:], 0.0)

        def open_banks():
            return [banks.tile([P, CH], F32, name="acc") for c in range(EB)]

        def add(accs, c, side, child, e):
            nc.tensor.matmul(
                accs[c][:],
                w_rows[side][e][:, c * P : (c + 1) * P],
                child[e][:],
                start=(side == 0 and e == 0),
                stop=(side == 1 and e == EB - 1),
            )

        def add_children(accs, left, right, e):
            if e < EB - 1:
                for side, child in enumerate((left, right)):
                    for c in range(EB):
                        add(accs, c, side, child, e)
            else:
                for c in range(EB):
                    for side, child in enumerate((left, right)):
                        add(accs, c, side, child, e)

        def finish_parent(accs, parent):
            for c in range(EB):
                nc.scalar.activation(parent[c][:], accs[c][:], FUNC.Relu, bias=wb[:, c : c + 1])

        def classify(nodes, first_column, last=False):
            parts = [(m, 0, CH) for m in range(MB)]
            if last:
                half, quarter = CH // 2, CH // 4
                parts = [(m, lo, half) for m in range(MB) for lo in (0, half)]
                parts[-1:] = [(MB - 1, lo, quarter) for lo in (half, half + quarter)]
            for part, (m, lo, width) in enumerate(parts):
                acc = banks.tile([P, width], F32, name="acc")
                for e in range(EB):
                    nc.tensor.matmul(
                        acc[:],
                        pw_blocks[:, e, m * P : (m + 1) * P],
                        nodes[e][:, lo : lo + width],
                        start=(e == 0),
                        stop=(e == EB - 1),
                    )
                scores = results.tile([P, width], F32, name="scores")
                if last and part % 2 == 1:
                    nc.vector.tensor_scalar_add(scores[:], acc[:], pb[:, m : m + 1])
                else:
                    nc.scalar.activation(scores[:], acc[:], FUNC.Identity, bias=pb[:, m : m + 1])
                nc.sync.dma_start(
                    out[m * P : (m + 1) * P, first_column + lo : first_column + lo + width], scores[:]
                )

        def leaves_to_h2(q, blocks):
            for c in blocks:
                look_up(q, c)
                look_up(q + G2, c)
            for e in blocks:
                if e == 0:
                    h2_banks[q] = open_banks()
                add_children(h2_banks[q], h1[q], h1[q + G2], e)

        for t in range(G3):
            h2_chunks = (t, t + G3)
            for i, g in enumerate((t, t + G2, t + G3, t + G3 + G2)):
                h1[g] = [held.tile([P, CH], BF16, name=f"h1_{i}_{e}") for e in range(EB)]
            for i, q in enumerate(h2_chunks):
                h2[q] = [held.tile([P, CH], BF16, name=f"h2_{i}_{e}") for e in range(EB)]
            h3[t] = [held.tile([P, CH], BF16, name=f"h3_{e}") for e in range(EB)]

            together = TOGETHER if t == 0 else 0
            for c in range(together):
                for q in h2_chunks:
                    leaves_to_h2(q, [c])
            for q in h2_chunks:
                leaves_to_h2(q, range(together, EB))
                finish_parent(h2_banks[q], h2[q])
                classify(h1[q], q * CH)
                classify(h1[q + G2], (q + G2) * CH)
                if q == t:
                    classify(h2[t], H1 + t * CH)
                    h3_banks = open_banks()
                    for e in range(EB):
                        for c in range(EB):
                            add(h3_banks, c, 0, h2[t], e)

            for e in range(EB):
                for c in range(EB):
                    add(h3_banks, c, 1, h2[t + G3], e)
            finish_parent(h3_banks, h3[t])
            classify(h2[t + G3], H1 + (t + G3) * CH)
            classify(h3[t], H1 + H2 + t * CH, last=(t == G3 - 1))
